import numpy as np
import ml_dtypes


def mxq(x, axis, fmt="e4m3"):
    dtype, down = {"e4m3": (ml_dtypes.float8_e4m3fn, 7), "e5m2": (ml_dtypes.float8_e5m2, 14)}[fmt]
    v = np.moveaxis(np.asarray(x, np.float32).astype(ml_dtypes.bfloat16).astype(np.float64), axis, -1)
    blocks = v.reshape(v.shape[:-1] + (-1, 32))
    amax = np.abs(blocks).max(-1, keepdims=True)
    byte = np.maximum(np.where(amax > 0, np.frexp(amax)[1] - 1 + 127, 0) - down, 1)
    scale = np.exp2(byte - 127.0)
    codes = (blocks / scale).astype(np.float32).astype(dtype).astype(np.float64)
    return np.moveaxis((codes * scale).reshape(v.shape), -1, axis)


WIDE = False


def mx_kscale(k):
    if not WIDE:
        return np.ones(k)
    levels = np.array([10, -10, 5, -5, 0])
    a = np.random.permutation(np.resize(levels, k // 512 * 4)).reshape(k // 512, 4)
    idx = np.arange(k)
    return np.exp2(a[idx // 512, idx % 128 // 32])


BF16 = ml_dtypes.bfloat16


def bf(x):
    return np.asarray(x, np.float32).astype(BF16)


def f64(x):
    return np.asarray(x).astype(np.float64)


B, CI, R, CO, H, W, D, K, PAD = 2, 512, 512, 128, 16, 16, 16, 3, 1
N = H * W * D


def setup_inputs():
    s, u = mx_kscale(CI), mx_kscale(R)
    return {"x": bf(np.random.standard_normal((B, CI, H, W, D)) * s[None, :, None, None, None]),
            "U_k_h": bf(np.random.standard_normal((K, R)) / np.sqrt(K)),
            "U_k_w": bf(np.random.standard_normal((K, R)) / np.sqrt(K)),
            "U_k_d": bf(np.random.standard_normal((K, R)) / np.sqrt(K)),
            "U_c_in": bf(np.random.standard_normal((CI, R)) / np.sqrt(CI) / s[:, None] * u[None, :]),
            "U_c_out": bf(np.random.standard_normal((R, CO)) / np.sqrt(R) / u[:, None]),
            "bias": bf(np.random.standard_normal(CO) * 0.5)}


def reference(x, U_k_h, U_k_w, U_k_d, U_c_in, U_c_out, bias):
    kh, kw, kd = f64(U_k_h), f64(U_k_w), f64(U_k_d)
    t = (mxq(f64(U_c_in), 0, "e4m3").T @ mxq(f64(x).reshape(B, CI, N), 1, "e4m3")).reshape(B, R, H, W, D)
    t = np.pad(t, ((0, 0), (0, 0), (PAD, PAD), (PAD, PAD), (PAD, PAD)))
    t = sum(t[:, :, k:k + H, :, :] * kh[k][None, :, None, None, None] for k in range(K))
    t = sum(t[:, :, :, k:k + W, :] * kw[k][None, :, None, None, None] for k in range(K))
    t = sum(t[:, :, :, :, k:k + D] * kd[k][None, :, None, None, None] for k in range(K))
    out = (mxq(f64(U_c_out), 0, "e4m3").T @ mxq(t.reshape(B, R, N), 1, "e4m3")).reshape(B, CO, H, W, D)
    return out + f64(bias)[None, :, None, None, None]

@@ -1,0 +1,284 @@
+import concourse.mybir as mybir
+from concourse.masks import make_identity
+
+F32 = mybir.dt.float32
+BF16 = mybir.dt.bfloat16
+U32 = mybir.dt.uint32
+U8 = mybir.dt.uint8
+FP8X4 = mybir.dt.float8_e4m3fn_x4
+MULT = mybir.AluOpType.mult
+ADD = mybir.AluOpType.add
+COPY = mybir.ActivationFunctionType.Copy
+IDENT = mybir.ActivationFunctionType.Identity
+
+P = 128
+B, CI, R, CO, H, W, D = 2, 512, 512, 128, 16, 16, 16
+SLAB = W * D
+NVOX = H * SLAB
+NT = R // P
+SL = 4
+CH = SL * SLAB
+NCH = B * H // SL
+NU = NCH * NT
+AHEAD = 8
+
+FLOPS = 2 * B * NVOX * R * (CI + CO) + 15 * B * NVOX * R
+
+FH, FW, FD = 0, 1, 2
+BIAS_COL = 36
+
+
+def tile_lowrankconv3d_pa_t_kernel(tc, x, U_k_h, U_k_w, U_k_d, U_c_in, U_c_out, bias, out):
+    nc = tc.nc
+    with tc.tile_pool(name="const", bufs=1) as const, tc.tile_pool(name="xraw", bufs=4) as xraw_pool, tc.tile_pool(
+        name="xg", bufs=4
+    ) as xg_pool, tc.tile_pool(name="acc", bufs=3) as acc_pool, tc.tile_pool(name="t3", bufs=4) as t3_pool, tc.tile_pool(
+        name="outp", bufs=3
+    ) as out_pool, tc.psum_pool(name="psp", bufs=6) as ps_p, tc.psum_pool(name="pso", bufs=2) as ps_o, tc.manual_schedule():
+
+        def regroup(engine_copy, dst, src):
+            engine_copy(
+                out=dst.rearrange("p (c i) j -> p c j i", i=4),
+                in_=src.rearrange("p j (c i) -> p c j i", i=4),
+            )
+
+        def quantise(codes, scales, grouped):
+            nc.vector.quantize_mx(
+                out=codes.bitcast(FP8X4), scales=scales, in_=grouped.rearrange("p n j -> p (n j)")
+            )
+
+        tap_rows = const.tile([P, P], BF16, name="tap_rows")
+        nc.vector.memset(tap_rows[:], 0.0)
+        ident = const.tile([P, P], BF16, name="ident")
+        make_identity(nc, ident[:])
+
+        uin_raw = const.tile([P, 4, R], BF16, name="uin_raw")
+        nc.sync.dma_start(out=uin_raw[:], in_=U_c_in.rearrange("(p j) r -> p j r", j=4))
+        xraw = {}
+
+        def load_x(c):
+            b, n0 = c // (NCH // B), (c % (NCH // B)) * CH
+            xraw[c] = xraw_pool.tile([P, 4, CH], BF16, name="xraw", tag="xraw")
+            nc.sync.dma_start(
+                out=xraw[c][:], in_=x[b].rearrange("(p j) h w d -> p j (h w d)", j=4)[:, :, n0 : n0 + CH]
+            )
+
+        for c in range(4):
+            load_x(c)
+
+        for f, taps_dram in enumerate((U_k_h, U_k_w, U_k_d)):
+            nc.scalar.dma_start(
+                out=tap_rows[12 * f : 12 * f + 12, :], in_=taps_dram.rearrange("k (t p) -> (k t) p", p=P)
+            )
+        nc.scalar.dma_start(out=tap_rows[BIAS_COL : BIAS_COL + 1, :], in_=bias.rearrange("(o c) -> o c", o=1))
+        uout_raw = const.tile([P, 4, CO], BF16, name="uout_raw")
+        nc.scalar.dma_start(out=uout_raw[:], in_=U_c_out.rearrange("(t p) o -> p t o", p=P))
+
+        uin_g = const.tile([P, R, 4], BF16, name="uin_g", align_bytes=64)
+        uin_codes = const.tile([P, R], U32, name="uin_codes", align_bytes=64)
+        uin_scales = const.tile([P, R], U8, name="uin_scales", align_bytes=64)
+        uout_g = const.tile([P, CO, 4], BF16, name="uout_g", align_bytes=64)
+        uout_codes = const.tile([P, CO], U32, name="uout_codes", align_bytes=64)
+        uout_scales = const.tile([P, CO], U8, name="uout_scales", align_bytes=64)
+        xcodes = [const.tile([P, NVOX], U32, name="xcodes%d" % b, align_bytes=64) for b in range(B)]
+        xscales = [const.tile([P, NVOX], U8, name="xscales%d" % b, align_bytes=64) for b in range(B)]
+        taps = const.tile([P, P], F32, name="taps")
+
+        def tap(f, k, t):
+            q = 12 * f + 4 * k + t
+            return taps[:, q : q + 1]
+
+        xg = {}
+
+        def x_regroup(g, engine_copy):
+            c, q = g // SL, g % SL
+            xg[g] = xg_pool.tile([P, SLAB, 4], BF16, name="xg", tag="xg", align_bytes=64)
+            regroup(engine_copy, xg[g][:], xraw[c][:, :, q * SLAB : (q + 1) * SLAB])
+
+        def x_quantise(g):
+            b, h = g // H, g % H
+            cols = slice(h * SLAB, (h + 1) * SLAB)
+            quantise(xcodes[b][:, cols], xscales[b][:, cols], xg[g][:])
+
+        bank = {}
+        acc1 = {}
+        acc2 = {}
+        acc3 = {}
+
+        def where(u):
+            c, t = u // NT, u % NT
+            return c, t, c // (NCH // B), (c % (NCH // B)) * SL
+
+        def mx1(u):
+            c, t, b, h0 = where(u)
+            rk = slice(t * P, (t + 1) * P)
+            for i in range(3):
+                first = h0 - 1 + 2 * i
+                lo, hi = max(first, 0), min(first + 1, H - 1)
+                n = (hi - lo + 1) * SLAB
+                off = (lo - first) * SLAB
+                bank[u, i] = ps_p.tile([P, 2 * SLAB], F32, name="bank", tag="bank")
+                nc.tensor.matmul_mx(
+                    out=bank[u, i][:, off : off + n],
+                    lhsT=uin_codes[:, rk].bitcast(FP8X4),
+                    lhsT_scale=uin_scales[:, rk],
+                    rhs=xcodes[b][:, lo * SLAB : lo * SLAB + n].bitcast(FP8X4),
+                    rhs_scale=xscales[b][:, lo * SLAB : lo * SLAB + n],
+                    start=True,
+                    stop=True,
+                )
+
+        def s_a(u):
+            c, t, b, h0 = where(u)
+            acc1[u] = acc_pool.tile([P, CH], F32, name="acc1", tag="acc1")
+            k = tap(FH, 1, t)
+            nc.scalar.activation(out=acc1[u][:, 0:SLAB], in_=bank[u, 0][:, SLAB : 2 * SLAB], func=COPY, scale=k)
+            nc.scalar.activation(out=acc1[u][:, SLAB : 3 * SLAB], in_=bank[u, 1][:, :], func=COPY, scale=k)
+            nc.scalar.activation(out=acc1[u][:, 3 * SLAB : 4 * SLAB], in_=bank[u, 2][:, 0:SLAB], func=COPY, scale=k)
+
+        def fma(dst, src, k):
+            nc.vector.scalar_tensor_tensor(out=dst, in0=src, scalar=k, in1=dst, op0=MULT, op1=ADD)
+
+        def v_a(u):
+            c, t, b, h0 = where(u)
+            a = acc1[u]
+            below, above = tap(FH, 0, t), tap(FH, 2, t)
+            if h0 == 0:
+                fma(a[:, SLAB : 2 * SLAB], bank[u, 0][:, SLAB : 2 * SLAB], below)
+            else:
+                fma(a[:, 0 : 2 * SLAB], bank[u, 0][:, :], below)
+            fma(a[:, 2 * SLAB : 4 * SLAB], bank[u, 1][:, :], below)
+            fma(a[:, 0 : 2 * SLAB], bank[u, 1][:, :], above)
+            if h0 + SL == H:
+                fma(a[:, 2 * SLAB : 3 * SLAB], bank[u, 2][:, 0:SLAB], above)
+            else:
+                fma(a[:, 2 * SLAB : 4 * SLAB], bank[u, 2][:, :], above)
+
+        def s_b(u):
+            c, t, b, h0 = where(u)
+            acc2[u] = acc_pool.tile([P, CH], F32, name="acc2", tag="acc2")
+            nc.scalar.activation(out=acc2[u][:], in_=acc1[u][:], func=COPY, scale=tap(FD, 1, t))
+
+        def v_b(u):
+            c, t, b, h0 = where(u)
+            src = acc1[u][:].rearrange("p (r d) -> p r d", d=D)
+            dst = acc2[u][:].rearrange("p (r d) -> p r d", d=D)
+            fma(dst[:, :, 1:D], src[:, :, 0 : D - 1], tap(FD, 0, t))
+            fma(dst[:, :, 0 : D - 1], src[:, :, 1:D], tap(FD, 2, t))
+
+        def s_c(u):
+            c, t, b, h0 = where(u)
+            if t == 0:
+                acc3[c] = acc_pool.tile([P, NT, CH], F32, name="acc3", tag="acc3")
+            nc.scalar.activation(out=acc3[c][:, t, :], in_=acc2[u][:], func=COPY, scale=tap(FW, 1, t))
+
+        def v_c(u):
+            c, t, b, h0 = where(u)
+            src = acc2[u][:].rearrange("p (h v) -> p h v", v=SLAB)
+            dst = acc3[c][:, t, :].rearrange("p (h v) -> p h v", v=SLAB)
+            fma(dst[:, :, D:SLAB], src[:, :, 0 : SLAB - D], tap(FW, 0, t))
+            fma(dst[:, :, 0 : SLAB - D], src[:, :, D:SLAB], tap(FW, 2, t))
+
+        g3 = {}
+        t3c = {}
+        t3s = {}
+        pso = {}
+        outsb = {}
+
+        def t3_regroup(c, j, engine_copy):
+            g3[c, j] = t3_pool.tile([P, SLAB, 4], BF16, name="g3", tag="g3", align_bytes=64)
+            regroup(engine_copy, g3[c, j][:], acc3[c][:, :, j * SLAB : (j + 1) * SLAB])
+
+        def t3_quantise(c, j):
+            t3c[c, j] = t3_pool.tile([P, SLAB], U32, name="t3c", tag="t3c", align_bytes=64)
+            t3s[c, j] = t3_pool.tile([P, SLAB], U8, name="t3s", tag="t3s", align_bytes=64)
+            quantise(t3c[c, j][:], t3s[c, j][:], g3[c, j][:])
+
+        def mx2(c, j):
+            pso[c, j] = ps_o.tile([P, SLAB], F32, name="pso", tag="pso")
+            nc.tensor.matmul_mx(
+                out=pso[c, j][:],
+                lhsT=uout_codes[:].bitcast(FP8X4),
+                lhsT_scale=uout_scales[:],
+                rhs=t3c[c, j][:].bitcast(FP8X4),
+                rhs_scale=t3s[c, j][:],
+                start=True,
+                stop=True,
+            )
+
+        def evacuate(c, j):
+            if j == 0:
+                outsb[c] = out_pool.tile([P, CH], F32, name="outsb", tag="outsb")
+            nc.scalar.activation(
+                out=outsb[c][:, j * SLAB : (j + 1) * SLAB],
+                in_=pso[c, j][:],
+                func=IDENT,
+                bias=taps[:, BIAS_COL : BIAS_COL + 1],
+                scale=1.0,
+            )
+
+        def store(c):
+            b, n0 = c // (NCH // B), (c % (NCH // B)) * CH
+            nc.sync.dma_start(out=out[b].rearrange("o h w d -> o (h w d)")[:, n0 : n0 + CH], in_=outsb[c][:])
+
+        vcopy = nc.vector.tensor_copy
+        scopy = nc.scalar.copy
+        regroup(vcopy, uin_g[:], uin_raw[:])
+        x_regroup(0, vcopy)
+        x_regroup(2, scopy)
+        quantise(uin_codes[:], uin_scales[:], uin_g[:])
+        x_regroup(1, vcopy)
+        x_quantise(0)
+        tap_ps = ps_o.tile([P, P], BF16, name="tap_ps", tag="pso")
+        nc.tensor.transpose(out=tap_ps[:], in_=tap_rows[:], identity=ident[:])
+        x_regroup(3, vcopy)
+        x_quantise(1)
+        x_quantise(2)
+        nc.vector.tensor_copy(out=taps[:], in_=tap_ps[:])
+        x_regroup(5, scopy)
+        x_regroup(4, vcopy)
+        x_quantise(3)
+        regroup(vcopy, uout_g[:], uout_raw[:])
+        x_quantise(4)
+        mx1(0)
+        s_a(0)
+        x_regroup(6, vcopy)
+        x_quantise(5)
+        x_regroup(7, scopy)
+        quantise(uout_codes[:], uout_scales[:], uout_g[:])
+        x_quantise(6)
+        mx1(1)
+
+        for i in range(NU + 7):
+            if i + 1 < NU:
+                s_a(i + 1)
+            if i < NU:
+                v_a(i)
+            if i + 2 < NU:
+                mx1(i + 2)
+            if i % 4 == 0 and 4 + i // 4 < NCH:
+                load_x(4 + i // 4)
+            g = AHEAD + i
+            if g < B * H:
+                x_regroup(g, scopy)
+            if g - 1 < B * H:
+                x_quantise(g - 1)
+            if i < NU:
+                s_b(i)
+            if 0 <= i - 1 < NU:
+                v_b(i - 1)
+            c, j = (i - 6) // 4, (i - 6) % 4
+            if 0 <= c < NCH:
+                t3_regroup(c, j, scopy)
+            c, j = (i - 7) // 4, (i - 7) % 4
+            if 0 <= c < NCH:
+                t3_quantise(c, j)
+                mx2(c, j)
+            if 0 <= i - 1 < NU:
+                s_c(i - 1)
+            if 0 <= i - 2 < NU:
+                v_c(i - 2)
+            if 0 <= c < NCH:
+                evacuate(c, j)
+                if j == 3:
+                    store(c)

@@ -53,18 +53,25 @@ def tile_lowrankconv3d_pa_t_kernel(tc, x, U_k_h, U_k_w, U_k_d, U_c_in, U_c_out, 
         make_identity(nc, ident[:])
 
         uin_raw = const.tile([P, 4, R], BF16, name="uin_raw")
-        nc.sync.dma_start(out=uin_raw[:], in_=U_c_in.rearrange("(p j) r -> p j r", j=4))
         xraw = {}
 
-        def load_x(c):
+        def load_x(c, pieces):
             b, n0 = c // (NCH // B), (c % (NCH // B)) * CH
-            xraw[c] = xraw_pool.tile([P, 4, CH], BF16, name="xraw", tag="xraw")
+            if pieces[0] == 0:
+                xraw[c] = xraw_pool.tile([P, 4, CH], BF16, name="xraw", tag="xraw")
+            lo, hi = pieces[0] * SLAB, (pieces[-1] + 1) * SLAB
             nc.sync.dma_start(
-                out=xraw[c][:], in_=x[b].rearrange("(p j) h w d -> p j (h w d)", j=4)[:, :, n0 : n0 + CH]
+                out=xraw[c][:, :, lo:hi],
+                in_=x[b].rearrange("(p j) h w d -> p j (h w d)", j=4)[:, :, n0 + lo : n0 + hi],
             )
 
-        for c in range(4):
-            load_x(c)
+        load_x(0, (0, 1))
+        nc.sync.dma_start(out=uin_raw[:], in_=U_c_in.rearrange("(p j) r -> p j r", j=4))
+        load_x(0, (2, 3))
+        load_x(1, (0, 1))
+        load_x(1, (2, 3))
+        load_x(2, (0, 1, 2, 3))
+        load_x(3, (0, 1, 2, 3))
 
         for f, taps_dram in enumerate((U_k_h, U_k_w, U_k_d)):
             nc.scalar.dma_start(
@@ -159,12 +166,14 @@ def tile_lowrankconv3d_pa_t_kernel(tc, x, U_k_h, U_k_w, U_k_d, U_c_in, U_c_out, 
             acc2[u] = acc_pool.tile([P, CH], F32, name="acc2", tag="acc2")
             nc.scalar.activation(out=acc2[u][:], in_=acc1[u][:], func=COPY, scale=tap(FD, 1, t))
 
-        def v_b(u):
+        def v_b(u, side):
             c, t, b, h0 = where(u)
             src = acc1[u][:].rearrange("p (r d) -> p r d", d=D)
             dst = acc2[u][:].rearrange("p (r d) -> p r d", d=D)
-            fma(dst[:, :, 1:D], src[:, :, 0 : D - 1], tap(FD, 0, t))
-            fma(dst[:, :, 0 : D - 1], src[:, :, 1:D], tap(FD, 2, t))
+            if side == 0:
+                fma(dst[:, :, 1:D], src[:, :, 0 : D - 1], tap(FD, 0, t))
+            else:
+                fma(dst[:, :, 0 : D - 1], src[:, :, 1:D], tap(FD, 2, t))
 
         def s_c(u):
             c, t, b, h0 = where(u)
@@ -172,12 +181,14 @@ def tile_lowrankconv3d_pa_t_kernel(tc, x, U_k_h, U_k_w, U_k_d, U_c_in, U_c_out, 
                 acc3[c] = acc_pool.tile([P, NT, CH], F32, name="acc3", tag="acc3")
             nc.scalar.activation(out=acc3[c][:, t, :], in_=acc2[u][:], func=COPY, scale=tap(FW, 1, t))
 
-        def v_c(u):
+        def v_c(u, side):
             c, t, b, h0 = where(u)
             src = acc2[u][:].rearrange("p (h v) -> p h v", v=SLAB)
             dst = acc3[c][:, t, :].rearrange("p (h v) -> p h v", v=SLAB)
-            fma(dst[:, :, D:SLAB], src[:, :, 0 : SLAB - D], tap(FW, 0, t))
-            fma(dst[:, :, 0 : SLAB - D], src[:, :, D:SLAB], tap(FW, 2, t))
+            if side == 0:
+                fma(dst[:, :, D:SLAB], src[:, :, 0 : SLAB - D], tap(FW, 0, t))
+            else:
+                fma(dst[:, :, 0 : SLAB - D], src[:, :, D:SLAB], tap(FW, 2, t))
 
         g3 = {}
         t3c = {}
@@ -194,8 +205,11 @@ def tile_lowrankconv3d_pa_t_kernel(tc, x, U_k_h, U_k_w, U_k_d, U_c_in, U_c_out, 
             t3s[c, j] = t3_pool.tile([P, SLAB], U8, name="t3s", tag="t3s", align_bytes=64)
             quantise(t3c[c, j][:], t3s[c, j][:], g3[c, j][:])
 
-        def mx2(c, j):
-            pso[c, j] = ps_o.tile([P, SLAB], F32, name="pso", tag="pso")
+        def mx2(c, j, spare_banks=False):
+            if spare_banks:
+                pso[c, j] = ps_p.tile([P, SLAB], F32, name="pso_end", tag="bank")
+            else:
+                pso[c, j] = ps_o.tile([P, SLAB], F32, name="pso", tag="pso")
             nc.tensor.matmul_mx(
                 out=pso[c, j][:],
                 lhsT=uout_codes[:].bitcast(FP8X4),
@@ -206,50 +220,55 @@ def tile_lowrankconv3d_pa_t_kernel(tc, x, U_k_h, U_k_w, U_k_d, U_c_in, U_c_out, 
                 stop=True,
             )
 
-        def evacuate(c, j):
+        def evacuate(c, j, on_vector=False):
             if j == 0:
                 outsb[c] = out_pool.tile([P, CH], F32, name="outsb", tag="outsb")
-            nc.scalar.activation(
-                out=outsb[c][:, j * SLAB : (j + 1) * SLAB],
-                in_=pso[c, j][:],
-                func=IDENT,
-                bias=taps[:, BIAS_COL : BIAS_COL + 1],
-                scale=1.0,
-            )
+            dst = outsb[c][:, j * SLAB : (j + 1) * SLAB]
+            if on_vector:
+                nc.vector.tensor_scalar(
+                    out=dst, in0=pso[c, j][:], scalar1=taps[:, BIAS_COL : BIAS_COL + 1], scalar2=None, op0=ADD
+                )
+            else:
+                nc.scalar.activation(
+                    out=dst, in_=pso[c, j][:], func=IDENT, bias=taps[:, BIAS_COL : BIAS_COL + 1], scale=1.0
+                )
 
-        def store(c):
+        def store(c, j0, j1):
             b, n0 = c // (NCH // B), (c % (NCH // B)) * CH
-            nc.sync.dma_start(out=out[b].rearrange("o h w d -> o (h w d)")[:, n0 : n0 + CH], in_=outsb[c][:])
+            nc.sync.dma_start(
+                out=out[b].rearrange("o h w d -> o (h w d)")[:, n0 + j0 * SLAB : n0 + j1 * SLAB],
+                in_=outsb[c][:, j0 * SLAB : j1 * SLAB],
+            )
 
         vcopy = nc.vector.tensor_copy
         scopy = nc.scalar.copy
-        regroup(vcopy, uin_g[:], uin_raw[:])
         x_regroup(0, vcopy)
-        x_regroup(2, scopy)
-        quantise(uin_codes[:], uin_scales[:], uin_g[:])
-        x_regroup(1, vcopy)
+        x_regroup(1, scopy)
+        regroup(vcopy, uin_g[:], uin_raw[:])
         x_quantise(0)
         tap_ps = ps_o.tile([P, P], BF16, name="tap_ps", tag="pso")
         nc.tensor.transpose(out=tap_ps[:], in_=tap_rows[:], identity=ident[:])
-        x_regroup(3, vcopy)
+        x_regroup(2, vcopy)
+        x_regroup(3, scopy)
+        quantise(uin_codes[:], uin_scales[:], uin_g[:])
         x_quantise(1)
-        x_quantise(2)
         nc.vector.tensor_copy(out=taps[:], in_=tap_ps[:])
-        x_regroup(5, scopy)
+        x_quantise(2)
         x_regroup(4, vcopy)
         x_quantise(3)
         regroup(vcopy, uout_g[:], uout_raw[:])
         x_quantise(4)
         mx1(0)
         s_a(0)
+        x_regroup(5, scopy)
         x_regroup(6, vcopy)
+        quantise(uout_codes[:], uout_scales[:], uout_g[:])
         x_quantise(5)
         x_regroup(7, scopy)
-        quantise(uout_codes[:], uout_scales[:], uout_g[:])
         x_quantise(6)
         mx1(1)
 
-        for i in range(NU + 7):
+        for i in range(NU + 2):
             if i + 1 < NU:
                 s_a(i + 1)
             if i < NU:
@@ -257,7 +276,7 @@ def tile_lowrankconv3d_pa_t_kernel(tc, x, U_k_h, U_k_w, U_k_d, U_c_in, U_c_out, 
             if i + 2 < NU:
                 mx1(i + 2)
             if i % 4 == 0 and 4 + i // 4 < NCH:
-                load_x(4 + i // 4)
+                load_x(4 + i // 4, (0, 1, 2, 3))
             g = AHEAD + i
             if g < B * H:
                 x_regroup(g, scopy)
@@ -266,19 +285,40 @@ def tile_lowrankconv3d_pa_t_kernel(tc, x, U_k_h, U_k_w, U_k_d, U_c_in, U_c_out, 
             if i < NU:
                 s_b(i)
             if 0 <= i - 1 < NU:
-                v_b(i - 1)
+                v_b(i - 1, 0)
+            if 0 <= i - 2 < NU:
+                v_c(i - 2, 0)
             c, j = (i - 6) // 4, (i - 6) % 4
-            if 0 <= c < NCH:
+            if c >= 0:
                 t3_regroup(c, j, scopy)
-            c, j = (i - 7) // 4, (i - 7) % 4
-            if 0 <= c < NCH:
-                t3_quantise(c, j)
-                mx2(c, j)
+            if 0 <= i - 1 < NU:
+                v_b(i - 1, 1)
+            cp, jp = (i - 7) // 4, (i - 7) % 4
+            if cp >= 0:
+                evacuate(cp, jp)
+                if jp == 3:
+                    store(cp, 0, 4)
             if 0 <= i - 1 < NU:
                 s_c(i - 1)
             if 0 <= i - 2 < NU:
-                v_c(i - 2)
-            if 0 <= c < NCH:
-                evacuate(c, j)
-                if j == 3:
-                    store(c)
+                v_c(i - 2, 1)
+            if c >= 0:
+                t3_quantise(c, j)
+                mx2(c, j)
+
+        last = NCH - 1
+        evacuate(last - 1, 3)
+        store(last - 1, 0, 4)
+        t3_regroup(last, 0, scopy)
+        t3_regroup(last, 1, vcopy)
+        t3_regroup(last, 2, scopy)
+        t3_regroup(last, 3, vcopy)
+        for j in range(4):
+            t3_quantise(last, j)
+            mx2(last, j, spare_banks=True)
+        evacuate(last, 0)
+        evacuate(last, 1, on_vector=True)
+        store(last, 0, 2)
+        evacuate(last, 2)
+        evacuate(last, 3, on_vector=True)
+        store(last, 2, 4)

@@ -26,6 +26,8 @@ FLOPS = 2 * B * NVOX * R * (CI + CO) + 15 * B * NVOX * R
 
 FH, FW, FD = 0, 1, 2
 BIAS_COL = 36
+HALF = 2 * SLAB
+ON_TENSOR = tuple(range(0, 30, 3))
 
 
 def tile_lowrankconv3d_pa_t_kernel(tc, x, U_k_h, U_k_w, U_k_d, U_c_in, U_c_out, bias, out):
@@ -34,7 +36,9 @@ def tile_lowrankconv3d_pa_t_kernel(tc, x, U_k_h, U_k_w, U_k_d, U_c_in, U_c_out, 
         name="xg", bufs=4
     ) as xg_pool, tc.tile_pool(name="acc", bufs=3) as acc_pool, tc.tile_pool(name="t3", bufs=4) as t3_pool, tc.tile_pool(
         name="outp", bufs=3
-    ) as out_pool, tc.psum_pool(name="psp", bufs=6) as ps_p, tc.psum_pool(name="pso", bufs=2) as ps_o, tc.manual_schedule():
+    ) as out_pool, tc.psum_pool(name="psp", bufs=6) as ps_p, tc.psum_pool(name="pso", bufs=1) as ps_o, tc.psum_pool(
+        name="psd", bufs=1
+    ) as ps_d, tc.manual_schedule():
 
         def regroup(engine_copy, dst, src):
             engine_copy(
@@ -51,6 +55,9 @@ def tile_lowrankconv3d_pa_t_kernel(tc, x, U_k_h, U_k_w, U_k_d, U_c_in, U_c_out, 
         nc.vector.memset(tap_rows[:], 0.0)
         ident = const.tile([P, P], BF16, name="ident")
         make_identity(nc, ident[:])
+        ident_f = const.tile([P, P], F32, name="ident_f")
+        make_identity(nc, ident_f[:])
+        diag = const.tile([P, 3, NT, P], F32, name="diag")
 
         uin_raw = const.tile([P, 4, R], BF16, name="uin_raw")
         xraw = {}
@@ -95,6 +102,10 @@ def tile_lowrankconv3d_pa_t_kernel(tc, x, U_k_h, U_k_w, U_k_d, U_c_in, U_c_out, 
             q = 12 * f + 4 * k + t
             return taps[:, q : q + 1]
 
+        def make_diag(t):
+            for k in range(3):
+                nc.scalar.activation(out=diag[:, k, t, :], in_=ident_f[:], func=COPY, scale=tap(FD, k, t))
+
         xg = {}
 
         def x_regroup(g, engine_copy):
@@ -111,6 +122,7 @@ def tile_lowrankconv3d_pa_t_kernel(tc, x, U_k_h, U_k_w, U_k_d, U_c_in, U_c_out, 
         acc1 = {}
         acc2 = {}
         acc3 = {}
+        pd = {}
 
         def where(u):
             c, t = u // NT, u % NT
@@ -161,15 +173,33 @@ def tile_lowrankconv3d_pa_t_kernel(tc, x, U_k_h, U_k_w, U_k_d, U_c_in, U_c_out, 
             else:
                 fma(a[:, 2 * SLAB : 4 * SLAB], bank[u, 2][:, :], above)
 
+        def first_col(u):
+            return HALF if u in ON_TENSOR else 0
+
+        def pe_b(u):
+            c, t, b, h0 = where(u)
+            pd[u] = ps_d.tile([P, HALF], F32, name="pd", tag="pd")
+            src = acc1[u][:, 0:HALF].rearrange("p (r d) -> p r d", d=D)
+            dst = pd[u][:].rearrange("p (r d) -> p r d", d=D)
+            nc.tensor.matmul(out=pd[u][:], lhsT=diag[:, 1, t, :], rhs=acc1[u][:, 0:HALF], start=True, stop=False)
+            nc.tensor.matmul(
+                out=dst[:, :, 1:D], lhsT=diag[:, 0, t, :], rhs=src[:, :, 0 : D - 1], start=False, stop=False
+            )
+            nc.tensor.matmul(
+                out=dst[:, :, 0 : D - 1], lhsT=diag[:, 2, t, :], rhs=src[:, :, 1:D], start=False, stop=True
+            )
+
         def s_b(u):
             c, t, b, h0 = where(u)
-            acc2[u] = acc_pool.tile([P, CH], F32, name="acc2", tag="acc2")
-            nc.scalar.activation(out=acc2[u][:], in_=acc1[u][:], func=COPY, scale=tap(FD, 1, t))
+            lo = first_col(u)
+            acc2[u] = acc_pool.tile([P, CH], F32, name="acc2", tag="acc2", bufs=4)
+            nc.scalar.activation(out=acc2[u][:, lo:CH], in_=acc1[u][:, lo:CH], func=COPY, scale=tap(FD, 1, t))
 
         def v_b(u, side):
             c, t, b, h0 = where(u)
-            src = acc1[u][:].rearrange("p (r d) -> p r d", d=D)
-            dst = acc2[u][:].rearrange("p (r d) -> p r d", d=D)
+            lo = first_col(u)
+            src = acc1[u][:, lo:CH].rearrange("p (r d) -> p r d", d=D)
+            dst = acc2[u][:, lo:CH].rearrange("p (r d) -> p r d", d=D)
             if side == 0:
                 fma(dst[:, :, 1:D], src[:, :, 0 : D - 1], tap(FD, 0, t))
             else:
@@ -179,16 +209,24 @@ def tile_lowrankconv3d_pa_t_kernel(tc, x, U_k_h, U_k_w, U_k_d, U_c_in, U_c_out, 
             c, t, b, h0 = where(u)
             if t == 0:
                 acc3[c] = acc_pool.tile([P, NT, CH], F32, name="acc3", tag="acc3")
-            nc.scalar.activation(out=acc3[c][:, t, :], in_=acc2[u][:], func=COPY, scale=tap(FW, 1, t))
+            lo = first_col(u)
+            if lo:
+                nc.scalar.activation(out=acc3[c][:, t, 0:lo], in_=pd[u][:], func=COPY, scale=tap(FW, 1, t))
+            nc.scalar.activation(out=acc3[c][:, t, lo:CH], in_=acc2[u][:, lo:CH], func=COPY, scale=tap(FW, 1, t))
 
         def v_c(u, side):
             c, t, b, h0 = where(u)
-            src = acc2[u][:].rearrange("p (h v) -> p h v", v=SLAB)
-            dst = acc3[c][:, t, :].rearrange("p (h v) -> p h v", v=SLAB)
-            if side == 0:
-                fma(dst[:, :, D:SLAB], src[:, :, 0 : SLAB - D], tap(FW, 0, t))
-            else:
-                fma(dst[:, :, 0 : SLAB - D], src[:, :, D:SLAB], tap(FW, 2, t))
+            lo = first_col(u)
+            parts = [(acc2[u][:, lo:CH], acc3[c][:, t, lo:CH])]
+            if lo:
+                parts.append((pd[u][:], acc3[c][:, t, 0:lo]))
+            for flat_src, flat_dst in parts:
+                src = flat_src.rearrange("p (h v) -> p h v", v=SLAB)
+                dst = flat_dst.rearrange("p (h v) -> p h v", v=SLAB)
+                if side == 0:
+                    fma(dst[:, :, D:SLAB], src[:, :, 0 : SLAB - D], tap(FW, 0, t))
+                else:
+                    fma(dst[:, :, 0 : SLAB - D], src[:, :, D:SLAB], tap(FW, 2, t))
 
         g3 = {}
         t3c = {}
@@ -259,6 +297,7 @@ def tile_lowrankconv3d_pa_t_kernel(tc, x, U_k_h, U_k_w, U_k_d, U_c_in, U_c_out, 
         regroup(vcopy, uout_g[:], uout_raw[:])
         x_quantise(4)
         mx1(0)
+        make_diag(0)
         s_a(0)
         x_regroup(5, scopy)
         x_regroup(6, vcopy)
@@ -268,7 +307,16 @@ def tile_lowrankconv3d_pa_t_kernel(tc, x, U_k_h, U_k_w, U_k_d, U_c_in, U_c_out, 
         x_quantise(6)
         mx1(1)
 
-        for i in range(NU + 2):
+        def piece(n):
+            return n // 4, n % 4
+
+        for i in range(NU + 3):
+            if 0 <= i - 2 < NU:
+                s_c(i - 2)
+            if 0 <= i - 1 < NU:
+                v_b(i - 1, 0)
+            if 0 <= i - 3 < NU:
+                v_c(i - 3, 0)
             if i + 1 < NU:
                 s_a(i + 1)
             if i < NU:
@@ -277,42 +325,41 @@ def tile_lowrankconv3d_pa_t_kernel(tc, x, U_k_h, U_k_w, U_k_d, U_c_in, U_c_out, 
                 mx1(i + 2)
             if i % 4 == 0 and 4 + i // 4 < NCH:
                 load_x(4 + i // 4, (0, 1, 2, 3))
+            if i < 3:
+                make_diag(3 - i)
             g = AHEAD + i
             if g < B * H:
                 x_regroup(g, scopy)
             if g - 1 < B * H:
                 x_quantise(g - 1)
+            if i >= 7:
+                t3_regroup(piece(i - 7)[0], piece(i - 7)[1], scopy)
+            if i >= 8:
+                c, j = piece(i - 8)
+                t3_quantise(c, j)
+                mx2(c, j)
             if i < NU:
                 s_b(i)
             if 0 <= i - 1 < NU:
-                v_b(i - 1, 0)
-            if 0 <= i - 2 < NU:
-                v_c(i - 2, 0)
-            c, j = (i - 6) // 4, (i - 6) % 4
-            if c >= 0:
-                t3_regroup(c, j, scopy)
-            if 0 <= i - 1 < NU:
                 v_b(i - 1, 1)
-            cp, jp = (i - 7) // 4, (i - 7) % 4
-            if cp >= 0:
-                evacuate(cp, jp)
-                if jp == 3:
-                    store(cp, 0, 4)
-            if 0 <= i - 1 < NU:
-                s_c(i - 1)
-            if 0 <= i - 2 < NU:
-                v_c(i - 2, 1)
-            if c >= 0:
-                t3_quantise(c, j)
-                mx2(c, j)
+            if 0 <= i - 3 < NU:
+                v_c(i - 3, 1)
+            if i in ON_TENSOR:
+                pe_b(i)
+            if i >= 8:
+                evacuate(c, j)
+                if j == 3:
+                    store(c, 0, 4)
 
         last = NCH - 1
-        evacuate(last - 1, 3)
-        store(last - 1, 0, 4)
         t3_regroup(last, 0, scopy)
         t3_regroup(last, 1, vcopy)
+        t3_quantise(last - 1, 3)
+        mx2(last - 1, 3)
         t3_regroup(last, 2, scopy)
         t3_regroup(last, 3, vcopy)
+        evacuate(last - 1, 3)
+        store(last - 1, 0, 4)
         for j in range(4):
             t3_quantise(last, j)
             mx2(last, j, spare_banks=True)

@@ -217,7 +217,10 @@ def tile_lowrankconv3d_pa_t_kernel(tc, x, U_k_h, U_k_w, U_k_d, U_c_in, U_c_out, 
         def v_c(u, side):
             c, t, b, h0 = where(u)
             lo = first_col(u)
-            parts = [(acc2[u][:, lo:CH], acc3[c][:, t, lo:CH])]
+            hi = HALF if (side == 1 and on_gpsimd(u)) else CH
+            parts = []
+            if lo < hi:
+                parts.append((acc2[u][:, lo:hi], acc3[c][:, t, lo:hi]))
             if lo:
                 parts.append((pd[u][:], acc3[c][:, t, 0:lo]))
             for flat_src, flat_dst in parts:
@@ -227,6 +230,16 @@ def tile_lowrankconv3d_pa_t_kernel(tc, x, U_k_h, U_k_w, U_k_d, U_c_in, U_c_out, 
                     fma(dst[:, :, D:SLAB], src[:, :, 0 : SLAB - D], tap(FW, 0, t))
                 else:
                     fma(dst[:, :, 0 : SLAB - D], src[:, :, D:SLAB], tap(FW, 2, t))
+
+        def on_gpsimd(u):
+            return u + 3 < NU
+
+        def g_c(u):
+            c, t, b, h0 = where(u)
+            src = acc2[u][:, HALF:CH].rearrange("p (h v) -> p h v", v=SLAB)[:, :, D:SLAB]
+            dst = acc3[c][:, t, HALF:CH].rearrange("p (h v) -> p h v", v=SLAB)[:, :, 0 : SLAB - D]
+            nc.gpsimd.tensor_scalar(out=src, in0=src, scalar1=tap(FW, 2, t), scalar2=0.0, op0=MULT, op1=ADD)
+            nc.gpsimd.tensor_tensor(out=dst, in0=dst, in1=src, op=ADD)
 
         g3 = {}
         t3c = {}
@@ -317,6 +330,8 @@ def tile_lowrankconv3d_pa_t_kernel(tc, x, U_k_h, U_k_w, U_k_d, U_c_in, U_c_out, 
                 v_b(i - 1, 0)
             if 0 <= i - 3 < NU:
                 v_c(i - 3, 0)
+                if on_gpsimd(i - 3):
+                    g_c(i - 3)
             if i + 1 < NU:
                 s_a(i + 1)
             if i < NU:

@@ -149,7 +149,7 @@ def tile_lowrankconv3d_pa_t_kernel(tc, x, U_k_h, U_k_w, U_k_d, U_c_in, U_c_out, 
 
         def s_a(u):
             c, t, b, h0 = where(u)
-            acc1[u] = acc_pool.tile([P, CH], F32, name="acc1", tag="acc1")
+            acc1[u] = acc_pool.tile([P, CH], F32, name="acc1", tag="acc1", bufs=4)
             k = tap(FH, 1, t)
             nc.scalar.activation(out=acc1[u][:, 0:SLAB], in_=bank[u, 0][:, SLAB : 2 * SLAB], func=COPY, scale=k)
             nc.scalar.activation(out=acc1[u][:, SLAB : 3 * SLAB], in_=bank[u, 1][:, :], func=COPY, scale=k)
@@ -232,7 +232,7 @@ def tile_lowrankconv3d_pa_t_kernel(tc, x, U_k_h, U_k_w, U_k_d, U_c_in, U_c_out, 
                     fma(dst[:, :, 0 : SLAB - D], src[:, :, D:SLAB], tap(FW, 2, t))
 
         def on_gpsimd(u):
-            return u + 3 < NU
+            return u + 4 < NU
 
         def g_c(u):
             c, t, b, h0 = where(u)
@@ -323,15 +323,15 @@ def tile_lowrankconv3d_pa_t_kernel(tc, x, U_k_h, U_k_w, U_k_d, U_c_in, U_c_out, 
         def piece(n):
             return n // 4, n % 4
 
-        for i in range(NU + 3):
-            if 0 <= i - 2 < NU:
-                s_c(i - 2)
-            if 0 <= i - 1 < NU:
-                v_b(i - 1, 0)
+        for i in range(NU + 4):
             if 0 <= i - 3 < NU:
-                v_c(i - 3, 0)
-                if on_gpsimd(i - 3):
-                    g_c(i - 3)
+                s_c(i - 3)
+            if 0 <= i - 2 < NU:
+                v_b(i - 2, 0)
+            if 0 <= i - 4 < NU:
+                v_c(i - 4, 0)
+                if on_gpsimd(i - 4):
+                    g_c(i - 4)
             if i + 1 < NU:
                 s_a(i + 1)
             if i < NU:
@@ -347,21 +347,21 @@ def tile_lowrankconv3d_pa_t_kernel(tc, x, U_k_h, U_k_w, U_k_d, U_c_in, U_c_out, 
                 x_regroup(g, scopy)
             if g - 1 < B * H:
                 x_quantise(g - 1)
-            if i >= 7:
-                t3_regroup(piece(i - 7)[0], piece(i - 7)[1], scopy)
             if i >= 8:
-                c, j = piece(i - 8)
+                t3_regroup(piece(i - 8)[0], piece(i - 8)[1], scopy)
+            if i >= 9:
+                c, j = piece(i - 9)
                 t3_quantise(c, j)
                 mx2(c, j)
-            if i < NU:
-                s_b(i)
             if 0 <= i - 1 < NU:
-                v_b(i - 1, 1)
-            if 0 <= i - 3 < NU:
-                v_c(i - 3, 1)
-            if i in ON_TENSOR:
-                pe_b(i)
-            if i >= 8:
+                s_b(i - 1)
+            if 0 <= i - 2 < NU:
+                v_b(i - 2, 1)
+            if 0 <= i - 4 < NU:
+                v_c(i - 4, 1)
+            if i - 1 in ON_TENSOR:
+                pe_b(i - 1)
+            if i >= 9:
                 evacuate(c, j)
                 if j == 3:
                     store(c, 0, 4)

@@ -20,14 +20,28 @@ SL = 4
 CH = SL * SLAB
 NCH = B * H // SL
 NU = NCH * NT
-AHEAD = 8
+X_PLAN = {
+    0: ((5, 1), (6, 2), (8, 2)),
+    1: ((10, 2),),
+    2: ((12, 2),),
+    3: ((14, 2),),
+    4: ((16, 2),),
+    5: ((18, 2),),
+    6: ((20, 2),),
+    7: ((22, 2),),
+    8: ((24, 2),),
+    12: ((26, 2),),
+    16: ((28, 2),),
+    20: ((30, 2),),
+}
+X_LOADS = {0: 4, 1: 5, 2: 6, 4: 7}
 
 FLOPS = 2 * B * NVOX * R * (CI + CO) + 15 * B * NVOX * R
 
 FH, FW, FD = 0, 1, 2
 BIAS_COL = 36
 HALF = 2 * SLAB
-ON_TENSOR = tuple(range(0, 30, 3))
+ON_TENSOR = tuple(range(0, 33, 3))
 
 
 def tile_lowrankconv3d_pa_t_kernel(tc, x, U_k_h, U_k_w, U_k_d, U_c_in, U_c_out, bias, out):
@@ -108,14 +122,14 @@ def tile_lowrankconv3d_pa_t_kernel(tc, x, U_k_h, U_k_w, U_k_d, U_c_in, U_c_out, 
 
         xg = {}
 
-        def x_regroup(g, engine_copy):
+        def x_regroup(g, engine_copy, n=1):
             c, q = g // SL, g % SL
-            xg[g] = xg_pool.tile([P, SLAB, 4], BF16, name="xg", tag="xg", align_bytes=64)
-            regroup(engine_copy, xg[g][:], xraw[c][:, :, q * SLAB : (q + 1) * SLAB])
+            xg[g] = xg_pool.tile([P, n * SLAB, 4], BF16, name="xg", tag="xg", align_bytes=64)
+            regroup(engine_copy, xg[g][:], xraw[c][:, :, q * SLAB : (q + n) * SLAB])
 
-        def x_quantise(g):
+        def x_quantise(g, n=1):
             b, h = g // H, g % H
-            cols = slice(h * SLAB, (h + 1) * SLAB)
+            cols = slice(h * SLAB, (h + n) * SLAB)
             quantise(xcodes[b][:, cols], xscales[b][:, cols], xg[g][:])
 
         bank = {}
@@ -312,12 +326,6 @@ def tile_lowrankconv3d_pa_t_kernel(tc, x, U_k_h, U_k_w, U_k_d, U_c_in, U_c_out, 
         mx1(0)
         make_diag(0)
         s_a(0)
-        x_regroup(5, scopy)
-        x_regroup(6, vcopy)
-        quantise(uout_codes[:], uout_scales[:], uout_g[:])
-        x_quantise(5)
-        x_regroup(7, scopy)
-        x_quantise(6)
         mx1(1)
 
         def piece(n):
@@ -338,15 +346,16 @@ def tile_lowrankconv3d_pa_t_kernel(tc, x, U_k_h, U_k_w, U_k_d, U_c_in, U_c_out, 
                 v_a(i)
             if i + 2 < NU:
                 mx1(i + 2)
-            if i % 4 == 0 and 4 + i // 4 < NCH:
-                load_x(4 + i // 4, (0, 1, 2, 3))
+            if i in X_LOADS:
+                load_x(X_LOADS[i], (0, 1, 2, 3))
             if i < 3:
                 make_diag(3 - i)
-            g = AHEAD + i
-            if g < B * H:
-                x_regroup(g, scopy)
-            if g - 1 < B * H:
-                x_quantise(g - 1)
+            for g, n in X_PLAN.get(i, ()):
+                x_regroup(g, scopy, n)
+            if i == 0:
+                quantise(uout_codes[:], uout_scales[:], uout_g[:])
+            for g, n in X_PLAN.get(i - 1, ()):
+                x_quantise(g, n)
             if i >= 8:
                 t3_regroup(piece(i - 8)[0], piece(i - 8)[1], scopy)
             if i >= 9:

@@ -20,21 +20,7 @@ SL = 4
 CH = SL * SLAB
 NCH = B * H // SL
 NU = NCH * NT
-X_PLAN = {
-    0: ((5, 1), (6, 2), (8, 2)),
-    1: ((10, 2),),
-    2: ((12, 2),),
-    3: ((14, 2),),
-    4: ((16, 2),),
-    5: ((18, 2),),
-    6: ((20, 2),),
-    7: ((22, 2),),
-    8: ((24, 2),),
-    12: ((26, 2),),
-    16: ((28, 2),),
-    20: ((30, 2),),
-}
-X_LOADS = {0: 4, 1: 5, 2: 6, 4: 7}
+AHEAD = 8
 
 FLOPS = 2 * B * NVOX * R * (CI + CO) + 15 * B * NVOX * R
 
@@ -122,14 +108,14 @@ def tile_lowrankconv3d_pa_t_kernel(tc, x, U_k_h, U_k_w, U_k_d, U_c_in, U_c_out, 
 
         xg = {}
 
-        def x_regroup(g, engine_copy, n=1):
+        def x_regroup(g, engine_copy):
             c, q = g // SL, g % SL
-            xg[g] = xg_pool.tile([P, n * SLAB, 4], BF16, name="xg", tag="xg", align_bytes=64)
-            regroup(engine_copy, xg[g][:], xraw[c][:, :, q * SLAB : (q + n) * SLAB])
+            xg[g] = xg_pool.tile([P, SLAB, 4], BF16, name="xg", tag="xg", align_bytes=64)
+            regroup(engine_copy, xg[g][:], xraw[c][:, :, q * SLAB : (q + 1) * SLAB])
 
-        def x_quantise(g, n=1):
+        def x_quantise(g):
             b, h = g // H, g % H
-            cols = slice(h * SLAB, (h + n) * SLAB)
+            cols = slice(h * SLAB, (h + 1) * SLAB)
             quantise(xcodes[b][:, cols], xscales[b][:, cols], xg[g][:])
 
         bank = {}
@@ -137,6 +123,7 @@ def tile_lowrankconv3d_pa_t_kernel(tc, x, U_k_h, U_k_w, U_k_d, U_c_in, U_c_out, 
         acc2 = {}
         acc3 = {}
         pd = {}
+        prod = {}
 
         def where(u):
             c, t = u // NT, u % NT
@@ -231,7 +218,7 @@ def tile_lowrankconv3d_pa_t_kernel(tc, x, U_k_h, U_k_w, U_k_d, U_c_in, U_c_out, 
         def v_c(u, side):
             c, t, b, h0 = where(u)
             lo = first_col(u)
-            hi = HALF if (side == 1 and on_gpsimd(u)) else CH
+            hi = first_gpsimd_col(u) if (side == 1 and on_gpsimd(u)) else CH
             parts = []
             if lo < hi:
                 parts.append((acc2[u][:, lo:hi], acc3[c][:, t, lo:hi]))
@@ -248,11 +235,32 @@ def tile_lowrankconv3d_pa_t_kernel(tc, x, U_k_h, U_k_w, U_k_d, U_c_in, U_c_out, 
         def on_gpsimd(u):
             return u + 4 < NU
 
+        def scalar_multiplies(u):
+            return on_gpsimd(u) and (u < 4 or u >= 20)
+
+        def first_gpsimd_col(u):
+            return SLAB if (scalar_multiplies(u) and u not in ON_TENSOR) else HALF
+
+        def upper_rows(flat):
+            return flat.rearrange("p (h v) -> p h v", v=SLAB)[:, :, D:SLAB]
+
+        def s_m(u):
+            c, t, b, h0 = where(u)
+            lo = first_gpsimd_col(u)
+            prod[u] = acc_pool.tile([P, CH], F32, name="prod", tag="prod", bufs=2)
+            nc.scalar.activation(
+                out=upper_rows(prod[u][:, lo:CH]), in_=upper_rows(acc2[u][:, lo:CH]), func=COPY, scale=tap(FW, 2, t)
+            )
+
         def g_c(u):
             c, t, b, h0 = where(u)
-            src = acc2[u][:, HALF:CH].rearrange("p (h v) -> p h v", v=SLAB)[:, :, D:SLAB]
-            dst = acc3[c][:, t, HALF:CH].rearrange("p (h v) -> p h v", v=SLAB)[:, :, 0 : SLAB - D]
-            nc.gpsimd.tensor_scalar(out=src, in0=src, scalar1=tap(FW, 2, t), scalar2=0.0, op0=MULT, op1=ADD)
+            lo = first_gpsimd_col(u)
+            dst = acc3[c][:, t, lo:CH].rearrange("p (h v) -> p h v", v=SLAB)[:, :, 0 : SLAB - D]
+            if scalar_multiplies(u):
+                src = upper_rows(prod[u][:, lo:CH])
+            else:
+                src = upper_rows(acc2[u][:, lo:CH])
+                nc.gpsimd.tensor_scalar(out=src, in0=src, scalar1=tap(FW, 2, t), scalar2=0.0, op0=MULT, op1=ADD)
             nc.gpsimd.tensor_tensor(out=dst, in0=dst, in1=src, op=ADD)
 
         g3 = {}
@@ -326,6 +334,12 @@ def tile_lowrankconv3d_pa_t_kernel(tc, x, U_k_h, U_k_w, U_k_d, U_c_in, U_c_out, 
         mx1(0)
         make_diag(0)
         s_a(0)
+        x_regroup(5, scopy)
+        x_regroup(6, vcopy)
+        quantise(uout_codes[:], uout_scales[:], uout_g[:])
+        x_quantise(5)
+        x_regroup(7, scopy)
+        x_quantise(6)
         mx1(1)
 
         def piece(n):
@@ -334,6 +348,8 @@ def tile_lowrankconv3d_pa_t_kernel(tc, x, U_k_h, U_k_w, U_k_d, U_c_in, U_c_out, 
         for i in range(NU + 4):
             if 0 <= i - 3 < NU:
                 s_c(i - 3)
+                if scalar_multiplies(i - 3):
+                    s_m(i - 3)
             if 0 <= i - 2 < NU:
                 v_b(i - 2, 0)
             if 0 <= i - 4 < NU:
@@ -346,16 +362,15 @@ def tile_lowrankconv3d_pa_t_kernel(tc, x, U_k_h, U_k_w, U_k_d, U_c_in, U_c_out, 
                 v_a(i)
             if i + 2 < NU:
                 mx1(i + 2)
-            if i in X_LOADS:
-                load_x(X_LOADS[i], (0, 1, 2, 3))
+            if i % 4 == 0 and 4 + i // 4 < NCH:
+                load_x(4 + i // 4, (0, 1, 2, 3))
             if i < 3:
                 make_diag(3 - i)
-            for g, n in X_PLAN.get(i, ()):
-                x_regroup(g, scopy, n)
-            if i == 0:
-                quantise(uout_codes[:], uout_scales[:], uout_g[:])
-            for g, n in X_PLAN.get(i - 1, ()):
-                x_quantise(g, n)
+            g = AHEAD + i
+            if g < B * H:
+                x_regroup(g, scopy)
+            if g - 1 < B * H:
+                x_quantise(g - 1)
             if i >= 8:
                 t3_regroup(piece(i - 8)[0], piece(i - 8)[1], scopy)
             if i >= 9:

import concourse.mybir as mybir
from concourse.masks import make_identity

F32 = mybir.dt.float32
BF16 = mybir.dt.bfloat16
U32 = mybir.dt.uint32
U8 = mybir.dt.uint8
FP8X4 = mybir.dt.float8_e4m3fn_x4
MULT = mybir.AluOpType.mult
ADD = mybir.AluOpType.add
COPY = mybir.ActivationFunctionType.Copy
IDENT = mybir.ActivationFunctionType.Identity

P = 128
B, CI, R, CO, H, W, D = 2, 512, 512, 128, 16, 16, 16
SLAB = W * D
NVOX = H * SLAB
NT = R // P
SL = 4
CH = SL * SLAB
NCH = B * H // SL
NU = NCH * NT
AHEAD = 8

FLOPS = 2 * B * NVOX * R * (CI + CO) + 15 * B * NVOX * R

FH, FW, FD = 0, 1, 2
BIAS_COL = 36
HALF = 2 * SLAB
ON_TENSOR = tuple(range(0, 33, 3))


def tile_lowrankconv3d_pa_t_kernel(tc, x, U_k_h, U_k_w, U_k_d, U_c_in, U_c_out, bias, out):
    nc = tc.nc
    with tc.tile_pool(name="const", bufs=1) as const, tc.tile_pool(name="xraw", bufs=4) as xraw_pool, tc.tile_pool(
        name="xg", bufs=4
    ) as xg_pool, tc.tile_pool(name="acc", bufs=3) as acc_pool, tc.tile_pool(name="t3", bufs=4) as t3_pool, tc.tile_pool(
        name="outp", bufs=3
    ) as out_pool, tc.psum_pool(name="psp", bufs=6) as ps_p, tc.psum_pool(name="pso", bufs=1) as ps_o, tc.psum_pool(
        name="psd", bufs=1
    ) as ps_d, tc.manual_schedule():

        def regroup(engine_copy, dst, src):
            engine_copy(
                out=dst.rearrange("p (c i) j -> p c j i", i=4),
                in_=src.rearrange("p j (c i) -> p c j i", i=4),
            )

        def quantise(codes, scales, grouped):
            nc.vector.quantize_mx(
                out=codes.bitcast(FP8X4), scales=scales, in_=grouped.rearrange("p n j -> p (n j)")
            )

        tap_rows = const.tile([P, P], BF16, name="tap_rows")
        nc.vector.memset(tap_rows[:], 0.0)
        ident = const.tile([P, P], BF16, name="ident")
        make_identity(nc, ident[:])
        ident_f = const.tile([P, P], F32, name="ident_f")
        make_identity(nc, ident_f[:])
        diag = const.tile([P, 3, NT, P], F32, name="diag")

        uin_raw = const.tile([P, 4, R], BF16, name="uin_raw")
        xraw = {}

        def load_x(c, pieces):
            b, n0 = c // (NCH // B), (c % (NCH // B)) * CH
            if pieces[0] == 0:
                xraw[c] = xraw_pool.tile([P, 4, CH], BF16, name="xraw", tag="xraw")
            lo, hi = pieces[0] * SLAB, (pieces[-1] + 1) * SLAB
            nc.sync.dma_start(
                out=xraw[c][:, :, lo:hi],
                in_=x[b].rearrange("(p j) h w d -> p j (h w d)", j=4)[:, :, n0 + lo : n0 + hi],
            )

        load_x(0, (0, 1))
        nc.sync.dma_start(out=uin_raw[:], in_=U_c_in.rearrange("(p j) r -> p j r", j=4))
        load_x(0, (2, 3))
        load_x(1, (0, 1))
        load_x(1, (2, 3))
        load_x(2, (0, 1, 2, 3))
        load_x(3, (0, 1, 2, 3))

        for f, taps_dram in enumerate((U_k_h, U_k_w, U_k_d)):
            nc.scalar.dma_start(
                out=tap_rows[12 * f : 12 * f + 12, :], in_=taps_dram.rearrange("k (t p) -> (k t) p", p=P)
            )
        nc.scalar.dma_start(out=tap_rows[BIAS_COL : BIAS_COL + 1, :], in_=bias.rearrange("(o c) -> o c", o=1))
        uout_raw = const.tile([P, 4, CO], BF16, name="uout_raw")
        nc.scalar.dma_start(out=uout_raw[:], in_=U_c_out.rearrange("(t p) o -> p t o", p=P))

        uin_g = const.tile([P, R, 4], BF16, name="uin_g", align_bytes=64)
        uin_codes = const.tile([P, R], U32, name="uin_codes", align_bytes=64)
        uin_scales = const.tile([P, R], U8, name="uin_scales", align_bytes=64)
        uout_g = const.tile([P, CO, 4], BF16, name="uout_g", align_bytes=64)
        uout_codes = const.tile([P, CO], U32, name="uout_codes", align_bytes=64)
        uout_scales = const.tile([P, CO], U8, name="uout_scales", align_bytes=64)
        xcodes = [const.tile([P, NVOX], U32, name="xcodes%d" % b, align_bytes=64) for b in range(B)]
        xscales = [const.tile([P, NVOX], U8, name="xscales%d" % b, align_bytes=64) for b in range(B)]
        taps = const.tile([P, P], F32, name="taps")

        def tap(f, k, t):
            q = 12 * f + 4 * k + t
            return taps[:, q : q + 1]

        def make_diag(t):
            for k in range(3):
                nc.scalar.activation(out=diag[:, k, t, :], in_=ident_f[:], func=COPY, scale=tap(FD, k, t))

        xg = {}

        def x_regroup(g, engine_copy):
            c, q = g // SL, g % SL
            xg[g] = xg_pool.tile([P, SLAB, 4], BF16, name="xg", tag="xg", align_bytes=64)
            regroup(engine_copy, xg[g][:], xraw[c][:, :, q * SLAB : (q + 1) * SLAB])

        def x_quantise(g):
            b, h = g // H, g % H
            cols = slice(h * SLAB, (h + 1) * SLAB)
            quantise(xcodes[b][:, cols], xscales[b][:, cols], xg[g][:])

        bank = {}
        acc1 = {}
        acc2 = {}
        acc3 = {}
        pd = {}
        prod = {}

        def where(u):
            c, t = u // NT, u % NT
            return c, t, c // (NCH // B), (c % (NCH // B)) * SL

        def mx1(u):
            c, t, b, h0 = where(u)
            rk = slice(t * P, (t + 1) * P)
            for i in range(3):
                first = h0 - 1 + 2 * i
                lo, hi = max(first, 0), min(first + 1, H - 1)
                n = (hi - lo + 1) * SLAB
                off = (lo - first) * SLAB
                bank[u, i] = ps_p.tile([P, 2 * SLAB], F32, name="bank", tag="bank")
                nc.tensor.matmul_mx(
                    out=bank[u, i][:, off : off + n],
                    lhsT=uin_codes[:, rk].bitcast(FP8X4),
                    lhsT_scale=uin_scales[:, rk],
                    rhs=xcodes[b][:, lo * SLAB : lo * SLAB + n].bitcast(FP8X4),
                    rhs_scale=xscales[b][:, lo * SLAB : lo * SLAB + n],
                    start=True,
                    stop=True,
                )

        def s_a(u):
            c, t, b, h0 = where(u)
            acc1[u] = acc_pool.tile([P, CH], F32, name="acc1", tag="acc1", bufs=4)
            k = tap(FH, 1, t)
            nc.scalar.activation(out=acc1[u][:, 0:SLAB], in_=bank[u, 0][:, SLAB : 2 * SLAB], func=COPY, scale=k)
            nc.scalar.activation(out=acc1[u][:, SLAB : 3 * SLAB], in_=bank[u, 1][:, :], func=COPY, scale=k)
            nc.scalar.activation(out=acc1[u][:, 3 * SLAB : 4 * SLAB], in_=bank[u, 2][:, 0:SLAB], func=COPY, scale=k)

        def fma(dst, src, k):
            nc.vector.scalar_tensor_tensor(out=dst, in0=src, scalar=k, in1=dst, op0=MULT, op1=ADD)

        def v_a(u):
            c, t, b, h0 = where(u)
            a = acc1[u]
            below, above = tap(FH, 0, t), tap(FH, 2, t)
            if h0 == 0:
                fma(a[:, SLAB : 2 * SLAB], bank[u, 0][:, SLAB : 2 * SLAB], below)
            else:
                fma(a[:, 0 : 2 * SLAB], bank[u, 0][:, :], below)
            fma(a[:, 2 * SLAB : 4 * SLAB], bank[u, 1][:, :], below)
            fma(a[:, 0 : 2 * SLAB], bank[u, 1][:, :], above)
            if h0 + SL == H:
                fma(a[:, 2 * SLAB : 3 * SLAB], bank[u, 2][:, 0:SLAB], above)
            else:
                fma(a[:, 2 * SLAB : 4 * SLAB], bank[u, 2][:, :], above)

        def first_col(u):
            return HALF if u in ON_TENSOR else 0

        def pe_b(u):
            c, t, b, h0 = where(u)
            pd[u] = ps_d.tile([P, HALF], F32, name="pd", tag="pd")
            src = acc1[u][:, 0:HALF].rearrange("p (r d) -> p r d", d=D)
            dst = pd[u][:].rearrange("p (r d) -> p r d", d=D)
            nc.tensor.matmul(out=pd[u][:], lhsT=diag[:, 1, t, :], rhs=acc1[u][:, 0:HALF], start=True, stop=False)
            nc.tensor.matmul(
                out=dst[:, :, 1:D], lhsT=diag[:, 0, t, :], rhs=src[:, :, 0 : D - 1], start=False, stop=False
            )
            nc.tensor.matmul(
                out=dst[:, :, 0 : D - 1], lhsT=diag[:, 2, t, :], rhs=src[:, :, 1:D], start=False, stop=True
            )

        def s_b(u):
            c, t, b, h0 = where(u)
            lo = first_col(u)
            acc2[u] = acc_pool.tile([P, CH], F32, name="acc2", tag="acc2", bufs=4)
            nc.scalar.activation(out=acc2[u][:, lo:CH], in_=acc1[u][:, lo:CH], func=COPY, scale=tap(FD, 1, t))

        def v_b(u, side):
            c, t, b, h0 = where(u)
            lo = first_col(u)
            src = acc1[u][:, lo:CH].rearrange("p (r d) -> p r d", d=D)
            dst = acc2[u][:, lo:CH].rearrange("p (r d) -> p r d", d=D)
            if side == 0:
                fma(dst[:, :, 1:D], src[:, :, 0 : D - 1], tap(FD, 0, t))
            else:
                fma(dst[:, :, 0 : D - 1], src[:, :, 1:D], tap(FD, 2, t))

        def s_c(u):
            c, t, b, h0 = where(u)
            if t == 0:
                acc3[c] = acc_pool.tile([P, NT, CH], F32, name="acc3", tag="acc3")
            lo = first_col(u)
            if lo:
                nc.scalar.activation(out=acc3[c][:, t, 0:lo], in_=pd[u][:], func=COPY, scale=tap(FW, 1, t))
            nc.scalar.activation(out=acc3[c][:, t, lo:CH], in_=acc2[u][:, lo:CH], func=COPY, scale=tap(FW, 1, t))

        def v_c(u, side):
            c, t, b, h0 = where(u)
            lo = first_col(u)
            hi = first_gpsimd_col(u) if (side == 1 and on_gpsimd(u)) else CH
            parts = []
            if lo < hi:
                parts.append((acc2[u][:, lo:hi], acc3[c][:, t, lo:hi]))
            if lo:
                parts.append((pd[u][:], acc3[c][:, t, 0:lo]))
            for flat_src, flat_dst in parts:
                src = flat_src.rearrange("p (h v) -> p h v", v=SLAB)
                dst = flat_dst.rearrange("p (h v) -> p h v", v=SLAB)
                if side == 0:
                    fma(dst[:, :, D:SLAB], src[:, :, 0 : SLAB - D], tap(FW, 0, t))
                else:
                    fma(dst[:, :, 0 : SLAB - D], src[:, :, D:SLAB], tap(FW, 2, t))

        def on_gpsimd(u):
            return u + 4 < NU

        def scalar_multiplies(u):
            return on_gpsimd(u) and (u < 4 or u >= 20)

        def first_gpsimd_col(u):
            return SLAB if (scalar_multiplies(u) and u not in ON_TENSOR) else HALF

        def upper_rows(flat):
            return flat.rearrange("p (h v) -> p h v", v=SLAB)[:, :, D:SLAB]

        def s_m(u):
            c, t, b, h0 = where(u)
            lo = first_gpsimd_col(u)
            prod[u] = acc_pool.tile([P, CH], F32, name="prod", tag="prod", bufs=2)
            nc.scalar.activation(
                out=upper_rows(prod[u][:, lo:CH]), in_=upper_rows(acc2[u][:, lo:CH]), func=COPY, scale=tap(FW, 2, t)
            )

        def g_c(u):
            c, t, b, h0 = where(u)
            lo = first_gpsimd_col(u)
            dst = acc3[c][:, t, lo:CH].rearrange("p (h v) -> p h v", v=SLAB)[:, :, 0 : SLAB - D]
            if scalar_multiplies(u):
                src = upper_rows(prod[u][:, lo:CH])
            else:
                src = upper_rows(acc2[u][:, lo:CH])
                nc.gpsimd.tensor_scalar(out=src, in0=src, scalar1=tap(FW, 2, t), scalar2=0.0, op0=MULT, op1=ADD)
            nc.gpsimd.tensor_tensor(out=dst, in0=dst, in1=src, op=ADD)

        g3 = {}
        t3c = {}
        t3s = {}
        pso = {}
        outsb = {}

        def t3_regroup(c, j, engine_copy):
            g3[c, j] = t3_pool.tile([P, SLAB, 4], BF16, name="g3", tag="g3", align_bytes=64)
            regroup(engine_copy, g3[c, j][:], acc3[c][:, :, j * SLAB : (j + 1) * SLAB])

        def t3_quantise(c, j):
            t3c[c, j] = t3_pool.tile([P, SLAB], U32, name="t3c", tag="t3c", align_bytes=64)
            t3s[c, j] = t3_pool.tile([P, SLAB], U8, name="t3s", tag="t3s", align_bytes=64)
            quantise(t3c[c, j][:], t3s[c, j][:], g3[c, j][:])

        def mx2(c, j, spare_banks=False):
            if spare_banks:
                pso[c, j] = ps_p.tile([P, SLAB], F32, name="pso_end", tag="bank")
            else:
                pso[c, j] = ps_o.tile([P, SLAB], F32, name="pso", tag="pso")
            nc.tensor.matmul_mx(
                out=pso[c, j][:],
                lhsT=uout_codes[:].bitcast(FP8X4),
                lhsT_scale=uout_scales[:],
                rhs=t3c[c, j][:].bitcast(FP8X4),
                rhs_scale=t3s[c, j][:],
                start=True,
                stop=True,
            )

        def evacuate(c, j, on_vector=False):
            if j == 0:
                outsb[c] = out_pool.tile([P, CH], F32, name="outsb", tag="outsb")
            dst = outsb[c][:, j * SLAB : (j + 1) * SLAB]
            if on_vector:
                nc.vector.tensor_scalar(
                    out=dst, in0=pso[c, j][:], scalar1=taps[:, BIAS_COL : BIAS_COL + 1], scalar2=None, op0=ADD
                )
            else:
                nc.scalar.activation(
                    out=dst, in_=pso[c, j][:], func=IDENT, bias=taps[:, BIAS_COL : BIAS_COL + 1], scale=1.0
                )

        def store(c, j0, j1):
            b, n0 = c // (NCH // B), (c % (NCH // B)) * CH
            nc.sync.dma_start(
                out=out[b].rearrange("o h w d -> o (h w d)")[:, n0 + j0 * SLAB : n0 + j1 * SLAB],
                in_=outsb[c][:, j0 * SLAB : j1 * SLAB],
            )

        vcopy = nc.vector.tensor_copy
        scopy = nc.scalar.copy
        x_regroup(0, vcopy)
        x_regroup(1, scopy)
        regroup(vcopy, uin_g[:], uin_raw[:])
        x_quantise(0)
        tap_ps = ps_o.tile([P, P], BF16, name="tap_ps", tag="pso")
        nc.tensor.transpose(out=tap_ps[:], in_=tap_rows[:], identity=ident[:])
        x_regroup(2, vcopy)
        x_regroup(3, scopy)
        quantise(uin_codes[:], uin_scales[:], uin_g[:])
        x_quantise(1)
        nc.vector.tensor_copy(out=taps[:], in_=tap_ps[:])
        x_quantise(2)
        x_regroup(4, vcopy)
        x_quantise(3)
        regroup(vcopy, uout_g[:], uout_raw[:])
        x_quantise(4)
        mx1(0)
        make_diag(0)
        s_a(0)
        x_regroup(5, scopy)
        x_regroup(6, vcopy)
        quantise(uout_codes[:], uout_scales[:], uout_g[:])
        x_quantise(5)
        x_regroup(7, scopy)
        x_quantise(6)
        mx1(1)

        def piece(n):
            return n // 4, n % 4

        for i in range(NU + 4):
            if 0 <= i - 3 < NU:
                s_c(i - 3)
                if scalar_multiplies(i - 3):
                    s_m(i - 3)
            if 0 <= i - 2 < NU:
                v_b(i - 2, 0)
            if 0 <= i - 4 < NU:
                v_c(i - 4, 0)
                if on_gpsimd(i - 4):
                    g_c(i - 4)
            if i + 1 < NU:
                s_a(i + 1)
            if i < NU:
                v_a(i)
            if i + 2 < NU:
                mx1(i + 2)
            if i % 4 == 0 and 4 + i // 4 < NCH:
                load_x(4 + i // 4, (0, 1, 2, 3))
            if i < 3:
                make_diag(3 - i)
            g = AHEAD + i
            if g < B * H:
                x_regroup(g, scopy)
            if g - 1 < B * H:
                x_quantise(g - 1)
            if i >= 8:
                t3_regroup(piece(i - 8)[0], piece(i - 8)[1], scopy)
            if i >= 9:
                c, j = piece(i - 9)
                t3_quantise(c, j)
                mx2(c, j)
            if 0 <= i - 1 < NU:
                s_b(i - 1)
            if 0 <= i - 2 < NU:
                v_b(i - 2, 1)
            if 0 <= i - 4 < NU:
                v_c(i - 4, 1)
            if i - 1 in ON_TENSOR:
                pe_b(i - 1)
            if i >= 9:
                evacuate(c, j)
                if j == 3:
                    store(c, 0, 4)

        last = NCH - 1
        t3_regroup(last, 0, scopy)
        t3_regroup(last, 1, vcopy)
        t3_quantise(last - 1, 3)
        mx2(last - 1, 3)
        t3_regroup(last, 2, scopy)
        t3_regroup(last, 3, vcopy)
        evacuate(last - 1, 3)
        store(last - 1, 0, 4)
        for j in range(4):
            t3_quantise(last, j)
            mx2(last, j, spare_banks=True)
        evacuate(last, 0)
        evacuate(last, 1, on_vector=True)
        store(last, 0, 2)
        evacuate(last, 2)
        evacuate(last, 3, on_vector=True)
        store(last, 2, 4)
